import numpy as np
import ml_dtypes


def mxq(x, axis, fmt="e4m3"):
    dtype, down = {"e4m3": (ml_dtypes.float8_e4m3fn, 7), "e5m2": (ml_dtypes.float8_e5m2, 14)}[fmt]
    v = np.moveaxis(np.asarray(x, np.float32).astype(ml_dtypes.bfloat16).astype(np.float64), axis, -1)
    blocks = v.reshape(v.shape[:-1] + (-1, 32))
    amax = np.abs(blocks).max(-1, keepdims=True)
    byte = np.maximum(np.where(amax > 0, np.frexp(amax)[1] - 1 + 127, 0) - down, 1)
    scale = np.exp2(byte - 127.0)
    codes = (blocks / scale).astype(np.float32).astype(dtype).astype(np.float64)
    return np.moveaxis((codes * scale).reshape(v.shape), -1, axis)


WIDE = False


def mx_kscale(k):
    if not WIDE:
        return np.ones(k)
    levels = np.array([10, -10, 5, -5, 0])
    if k % 512:
        return np.exp2(np.random.permutation(np.resize(levels, k // 32))).repeat(32)
    a = np.empty((k // 512, 16))
    for p in range(k // 512):
        a[p, :8] = np.random.permutation(np.resize(levels, 8))
        for g in range(8):
            far = levels[np.abs(levels - a[p, g]) >= 10]
            a[p, g + 8] = far[np.random.randint(len(far))]
    return np.exp2(a.ravel()).repeat(32)


BF16 = ml_dtypes.bfloat16


def bf(x):
    return np.asarray(x, np.float32).astype(BF16)


def f64(x):
    return np.asarray(x).astype(np.float64)


B, S, C, HD = 1, 512, 3072, 128
H = C // HD
HP = HD // 2
EPS = 1e-6
THETA = 10000.0


def rmsnorm(h, g):
    return h * (1.0 / np.sqrt(np.mean(h * h, axis=-1, keepdims=True) + EPS)) * g


def apply_rope1(h, freqs):
    sh = h.shape
    h_ = h.reshape(*sh[:-1], -1, 1, 2)
    out = freqs[..., 0] * h_[..., 0] + freqs[..., 1] * h_[..., 1]
    return out.reshape(sh)


def setup_inputs():
    s = mx_kscale(C)
    pos = f64(np.random.randint(0, S, size=(S, 1)))
    inv_freq = 1.0 / THETA ** (np.arange(HP) / HP)
    ang = pos * inv_freq
    cos, sin = np.cos(ang), np.sin(ang)
    rot = np.stack([np.stack([cos, -sin], -1), np.stack([sin, cos], -1)], -2)
    return {"x": bf(np.random.standard_normal((B, S, C)) * s),
            "freqs": bf(rot[None, :, None]),
            "w": bf(np.random.standard_normal((C, C)) / np.sqrt(C) / s[None, :]),
            "b": bf(np.random.standard_normal(C) * 0.3),
            "g": bf(1.0 + 0.1 * np.random.standard_normal(HD))}


def reference(x, freqs, w, b, g):
    p = (mxq(f64(x), 2, "e4m3") @ mxq(f64(w), 1, "e4m3").T) + f64(b)
    h = p.reshape(B, S, H, HD)
    return apply_rope1(rmsnorm(h, f64(g)), f64(freqs))

@@ -1,0 +1,301 @@
+from contextlib import ExitStack
+
+import concourse.mybir as mybir
+from concourse.masks import make_identity
+
+F32 = mybir.dt.float32
+BF16 = mybir.dt.bfloat16
+U32 = mybir.dt.uint32
+U8 = mybir.dt.uint8
+FP8X4 = mybir.dt.float8_e4m3fn_x4
+ACT = mybir.ActivationFunctionType
+ALU = mybir.AluOpType
+
+P = 128
+TOKENS = 512
+CHANNELS = 3072
+HEAD = 128
+PAIRS = HEAD // 2
+EPS = 1e-6
+
+K_PASS = 4 * P
+PASSES = CHANNELS // K_PASS
+WORDS = K_PASS // 2
+BLOCK = 2 * P
+X_BLOCKS = TOKENS // BLOCK
+W_BLOCKS = CHANNELS // BLOCK
+HEADS_IN_BLOCK = BLOCK // HEAD
+HALF = PASSES // 2
+RAW_BUFS = 12
+PREPARATIONS = 2 * (X_BLOCKS + W_BLOCKS)
+BANKS = X_BLOCKS * W_BLOCKS
+GROUPS = 2 * HEADS_IN_BLOCK
+
+REGROUP_LAG = 1
+QUANTISE_LAG = 2
+MULTIPLY_LAG = 2 * X_BLOCKS + 2 + QUANTISE_LAG
+BIAS_LAG = 1
+PRODUCT_LAG = 2
+ADD_LAG = 3
+STORE_LAG = 4
+STEPS = BANKS + MULTIPLY_LAG + STORE_LAG
+
+FLOPS = 2 * TOKENS * CHANNELS * CHANNELS
+
+
+def tile_selfattention_pa_kernel(tc, x, freqs, w, b, g, out):
+    nc = tc.nc
+    x_rows = x.rearrange("o s k -> (o s) k")
+    freqs_view = freqs.rearrange("o (m p) q j i c -> p (o m q) (j i c)", p=P)
+    out_view = out.rearrange("o (m p) h d -> p (o m) (h d)", p=P)
+
+    blocks = [("x", 0), ("w", 0), ("x", 1)] + [("w", i) for i in range(1, W_BLOCKS)]
+    bank_of_step = {n + MULTIPLY_LAG - max(0, 2 - n): n for n in range(BANKS)}
+
+    with ExitStack() as ctx:
+        ctx.enter_context(tc.manual_schedule())
+        consts = ctx.enter_context(tc.tile_pool(name="consts", bufs=1))
+        raw_pool = ctx.enter_context(tc.tile_pool(name="raw", bufs=RAW_BUFS))
+        grouped_pool = ctx.enter_context(tc.tile_pool(name="grouped", bufs=3 * HALF))
+        x_mx = ctx.enter_context(tc.tile_pool(name="x_mx", bufs=1))
+        w_mx = ctx.enter_context(tc.tile_pool(name="w_mx", bufs=3))
+        work = ctx.enter_context(tc.tile_pool(name="work", bufs=3))
+        stats = ctx.enter_context(tc.tile_pool(name="stats", bufs=4))
+        flipped_psum = ctx.enter_context(tc.psum_pool(name="flipped_psum", bufs=2 * HALF))
+        acc_psum = ctx.enter_context(tc.psum_pool(name="acc_psum", bufs=2))
+
+        raw_tiles = {}
+        flipped_banks = {}
+        grouped_tiles = {}
+        mx_operands = {}
+        acc_banks = {}
+        biased = {}
+        square_sums = {}
+        rms_values = {}
+        inverse_rms = {}
+        product_tiles = {}
+        rotated_tiles = {}
+
+        def load(n):
+            if n < PREPARATIONS:
+                kind, i = blocks[n // 2]
+                rows = (x_rows if kind == "x" else w)[i * BLOCK : (i + 1) * BLOCK, :]
+                first = (n % 2) * HALF * K_PASS
+                raw = raw_pool.tile([P, 2, HALF * K_PASS], BF16, name="raw")
+                nc.sync.dma_start(
+                    out=raw[:],
+                    in_=rows[:, first : first + HALF * K_PASS].rearrange("(c p) k -> p c k", p=P),
+                )
+                raw_tiles[n] = raw
+
+        for n in range(4):
+            load(n)
+
+        eps = consts.tile([P, 1], F32, name="eps")
+        nc.vector.memset(eps[:], EPS)
+        warm = consts.tile([P, 1], F32, name="warm")
+        nc.scalar.activation(out=warm[:], in_=eps[:], func=ACT.Sqrt)
+        ident = consts.tile([P, P], F32, name="ident")
+        make_identity(nc, ident[:])
+
+        freqs_sb = consts.tile([P, TOKENS // P, 4 * PAIRS], BF16, name="freqs_sb")
+        nc.sync.dma_start(out=freqs_sb[:], in_=freqs_view)
+        gain = consts.tile([P, HEAD], BF16, name="gain")
+        nc.sync.dma_start(out=gain[:], in_=g.partition_broadcast(P))
+        bias = consts.tile([P, CHANNELS], BF16, name="bias")
+        nc.sync.dma_start(out=bias[:], in_=b.partition_broadcast(P))
+        for n in range(4, RAW_BUFS):
+            load(n)
+
+        table = []
+
+        def build_tables():
+            for c in range(2):
+                tab = consts.tile([P, TOKENS // P, PAIRS, 2], F32, name="table%d" % c)
+                nc.vector.tensor_tensor(
+                    out=tab[:],
+                    in0=freqs_sb[:].rearrange("p m (j i c) -> p c m j i", i=2, c=2)[:, c],
+                    in1=gain[:]
+                    .rearrange("p (j c) -> p c j", c=2)[:, c]
+                    .unsqueeze(1)
+                    .unsqueeze(3)
+                    .to_broadcast([P, TOKENS // P, PAIRS, 2]),
+                    op=ALU.mult,
+                )
+                table.append(tab)
+
+        def passes_of(n):
+            return range((n % 2) * HALF, (n % 2 + 1) * HALF)
+
+        def transpose(n):
+            if not 0 <= n < PREPARATIONS:
+                return
+            words = raw_tiles.pop(n)[:].bitcast(F32)
+            flipped_banks[n] = []
+            for local in range(HALF):
+                flipped = flipped_psum.tile([P, 2, BLOCK], F32, name="flipped")
+                for c in range(2):
+                    for u in range(2):
+                        nc.tensor.transpose(
+                            flipped[:, u, c * P : (c + 1) * P],
+                            words[:, c, local * WORDS + u : (local + 1) * WORDS : 2],
+                            ident[:],
+                        )
+                flipped_banks[n].append(flipped)
+            load(n + RAW_BUFS)
+
+        def regroup(n):
+            if not 0 <= n < PREPARATIONS:
+                return
+            grouped_tiles[n] = []
+            for flipped in flipped_banks.pop(n):
+                grouped = grouped_pool.tile([P, 4 * BLOCK], BF16, name="grouped", align_bytes=64)
+                nc.scalar.copy(
+                    out=grouped[:].bitcast(F32).rearrange("p (r u) -> p r u", u=2),
+                    in_=flipped[:].rearrange("p u r -> p r u"),
+                )
+                grouped_tiles[n].append(grouped)
+
+        def quantise(n):
+            if not 0 <= n < PREPARATIONS:
+                return
+            block = blocks[n // 2]
+            if n % 2 == 0:
+                pool, name = (x_mx, "x%d" % block[1]) if block[0] == "x" else (w_mx, "w")
+                codes = pool.tile([P, PASSES, BLOCK], U32, name=name + "_codes", align_bytes=64)
+                scales = pool.tile([P, PASSES, BLOCK], U8, name=name + "_scales", align_bytes=64)
+                mx_operands[block] = (codes, scales)
+            codes, scales = mx_operands[block]
+            for q, grouped in zip(passes_of(n), grouped_tiles.pop(n)):
+                nc.vector.quantize_mx(
+                    out=codes[:, q, :].bitcast(FP8X4), scales=scales[:, q, :], in_=grouped[:]
+                )
+
+        def multiply(n):
+            if n is None:
+                return
+            x_codes, x_scales = mx_operands[("x", n % X_BLOCKS)]
+            w_codes, w_scales = mx_operands[("w", n // X_BLOCKS)]
+            acc = acc_psum.tile([P, 2, BLOCK], F32, name="acc")
+            for c in range(2):
+                for q in range(PASSES):
+                    nc.tensor.matmul_mx(
+                        out=acc[:, c, :],
+                        lhsT=x_codes[:, q, c * P : (c + 1) * P].bitcast(FP8X4),
+                        lhsT_scale=x_scales[:, q, c * P : (c + 1) * P],
+                        rhs=w_codes[:, q, :].bitcast(FP8X4),
+                        rhs_scale=w_scales[:, q, :],
+                        start=(q == 0),
+                        stop=(q == PASSES - 1),
+                    )
+            acc_banks[n] = acc
+
+        def add_bias(n):
+            if n is None:
+                return
+            wb = n // X_BLOCKS
+            u = work.tile([P, 2, BLOCK], F32, name="u")
+            nc.vector.tensor_tensor(
+                out=u[:],
+                in0=acc_banks.pop(n)[:],
+                in1=bias[:, wb * BLOCK : (wb + 1) * BLOCK].unsqueeze(1).to_broadcast([P, 2, BLOCK]),
+                op=ALU.add,
+            )
+            biased[n] = u
+
+        def sum_squares(n):
+            if n is None:
+                return
+            by_group = biased.pop(n)[:].rearrange("p c (h d) -> p (c h) d", d=HEAD)
+            squares = work.tile([P, GROUPS, HEAD], F32, name="squares")
+            sums = stats.tile([P, GROUPS], F32, name="sums")
+            for k in range(GROUPS):
+                nc.scalar.activation(
+                    out=squares[:, k, :], in_=by_group[:, k, :], func=ACT.Square,
+                    accum_out=sums[:, k : k + 1],
+                )
+            square_sums[n] = sums
+
+        def root(n):
+            if n is None:
+                return
+            rms = stats.tile([P, GROUPS], F32, name="rms")
+            nc.scalar.activation(
+                out=rms[:], in_=square_sums.pop(n)[:], func=ACT.Sqrt, scale=1.0 / HEAD, bias=eps[:]
+            )
+            rms_values[n] = rms
+
+        def multiply_by_tables(n):
+            if n is None:
+                return
+            xb = n % X_BLOCKS
+            shape = [P, 2, HEADS_IN_BLOCK, PAIRS, 2]
+            pairs = biased[n][:].rearrange("p c (h j i) -> p c h j i", h=HEADS_IN_BLOCK, i=2)
+            product_tiles[n] = []
+            for c in range(2):
+                product = work.tile(shape, F32, name="product%d" % c)
+                nc.vector.tensor_tensor(
+                    out=product[:],
+                    in0=pairs[:, :, :, :, c : c + 1].to_broadcast(shape),
+                    in1=table[c][:, 2 * xb : 2 * xb + 2].unsqueeze(2).to_broadcast(shape),
+                    op=ALU.mult,
+                )
+                product_tiles[n].append(product)
+
+        def add_products(n):
+            if n is None:
+                return
+            first, second = product_tiles.pop(n)
+            rotated = work.tile([P, GROUPS, HEAD], F32, name="rotated")
+            nc.vector.tensor_tensor(
+                out=rotated[:].rearrange("p k d -> p (k d)"),
+                in0=first[:].rearrange("p c h j i -> p (c h j i)"),
+                in1=second[:].rearrange("p c h j i -> p (c h j i)"),
+                op=ALU.add,
+            )
+            rotated_tiles[n] = rotated
+
+        def invert(n):
+            if n is None:
+                return
+            inv_rms = stats.tile([P, GROUPS], F32, name="inv_rms")
+            nc.vector.reciprocal(out=inv_rms[:], in_=rms_values.pop(n)[:])
+            inverse_rms[n] = inv_rms
+
+        def scale_and_store(n):
+            if n is None:
+                return
+            xb, wb = n % X_BLOCKS, n // X_BLOCKS
+            rotated, inv_rms = rotated_tiles.pop(n), inverse_rms.pop(n)
+            result = work.tile([P, GROUPS, HEAD], F32, name="result")
+            for k in range(GROUPS):
+                nc.scalar.activation(
+                    out=result[:, k, :], in_=rotated[:, k, :], func=ACT.Copy, scale=inv_rms[:, k : k + 1]
+                )
+            nc.sync.dma_start(
+                out=out_view[:, 2 * xb : 2 * xb + 2, wb * BLOCK : (wb + 1) * BLOCK],
+                in_=result[:].rearrange("p (c h) d -> p c (h d)", c=2),
+            )
+
+        def step(t):
+            add_bias(bank_of_step.get(t - BIAS_LAG))
+            regroup(t - REGROUP_LAG)
+            if t % 2 == 0:
+                multiply(bank_of_step.get(t))
+                multiply(bank_of_step.get(t + 1))
+                transpose(t)
+                transpose(t + 1)
+            quantise(t - QUANTISE_LAG)
+            multiply_by_tables(bank_of_step.get(t - PRODUCT_LAG))
+            sum_squares(bank_of_step.get(t - PRODUCT_LAG))
+            add_products(bank_of_step.get(t - ADD_LAG))
+            invert(bank_of_step.get(t - ADD_LAG))
+            scale_and_store(bank_of_step.get(t - STORE_LAG))
+            root(bank_of_step.get(t - PRODUCT_LAG))
+
+        first_multiply = min(bank_of_step)
+        for t in range(first_multiply):
+            step(t)
+        build_tables()
+        for t in range(first_multiply, STEPS):
+            step(t)

@@ -280,11 +280,8 @@ def tile_selfattention_pa_kernel(tc, x, freqs, w, b, g, out):
         def step(t):
             add_bias(bank_of_step.get(t - BIAS_LAG))
             regroup(t - REGROUP_LAG)
-            if t % 2 == 0:
-                multiply(bank_of_step.get(t))
-                multiply(bank_of_step.get(t + 1))
-                transpose(t)
-                transpose(t + 1)
+            multiply(bank_of_step.get(t))
+            transpose(t)
             quantise(t - QUANTISE_LAG)
             multiply_by_tables(bank_of_step.get(t - PRODUCT_LAG))
             sum_squares(bank_of_step.get(t - PRODUCT_LAG))

@@ -26,6 +26,7 @@ X_BLOCKS = TOKENS // BLOCK
 W_BLOCKS = CHANNELS // BLOCK
 HEADS_IN_BLOCK = BLOCK // HEAD
 HALF = PASSES // 2
+FIRST_SPREAD = 4
 RAW_BUFS = 12
 PREPARATIONS = 2 * (X_BLOCKS + W_BLOCKS)
 BANKS = X_BLOCKS * W_BLOCKS
@@ -59,19 +60,20 @@ def tile_selfattention_pa_kernel(tc, x, freqs, w, b, g, out):
         grouped_pool = ctx.enter_context(tc.tile_pool(name="grouped", bufs=3 * HALF))
         x_mx = ctx.enter_context(tc.tile_pool(name="x_mx", bufs=1))
         w_mx = ctx.enter_context(tc.tile_pool(name="w_mx", bufs=3))
+        spread_pool = ctx.enter_context(tc.tile_pool(name="spread", bufs=3))
         work = ctx.enter_context(tc.tile_pool(name="work", bufs=3))
         stats = ctx.enter_context(tc.tile_pool(name="stats", bufs=4))
         flipped_psum = ctx.enter_context(tc.psum_pool(name="flipped_psum", bufs=2 * HALF))
         acc_psum = ctx.enter_context(tc.psum_pool(name="acc_psum", bufs=2))
 
         raw_tiles = {}
+        spread_tiles = {}
         flipped_banks = {}
         grouped_tiles = {}
         mx_operands = {}
         acc_banks = {}
         biased = {}
         square_sums = {}
-        rms_values = {}
         inverse_rms = {}
         product_tiles = {}
         rotated_tiles = {}
@@ -82,19 +84,21 @@ def tile_selfattention_pa_kernel(tc, x, freqs, w, b, g, out):
                 rows = (x_rows if kind == "x" else w)[i * BLOCK : (i + 1) * BLOCK, :]
                 first = (n % 2) * HALF * K_PASS
                 raw = raw_pool.tile([P, 2, HALF * K_PASS], BF16, name="raw")
-                nc.sync.dma_start(
-                    out=raw[:],
-                    in_=rows[:, first : first + HALF * K_PASS].rearrange("(c p) k -> p c k", p=P),
-                )
+                width = K_PASS if n == 0 else HALF * K_PASS
+                for k in range(0, HALF * K_PASS, width):
+                    nc.sync.dma_start(
+                        out=raw[:, :, k : k + width],
+                        in_=rows[:, first + k : first + k + width].rearrange("(c p) k -> p c k", p=P),
+                    )
                 raw_tiles[n] = raw
 
-        for n in range(4):
+        for n in range(6):
             load(n)
 
         eps = consts.tile([P, 1], F32, name="eps")
         nc.vector.memset(eps[:], EPS)
         warm = consts.tile([P, 1], F32, name="warm")
-        nc.scalar.activation(out=warm[:], in_=eps[:], func=ACT.Sqrt)
+        nc.scalar.activation(out=warm[:], in_=eps[:], func=ACT.Abs_reciprocal_sqrt)
         ident = consts.tile([P, P], F32, name="ident")
         make_identity(nc, ident[:])
 
@@ -103,9 +107,15 @@ def tile_selfattention_pa_kernel(tc, x, freqs, w, b, g, out):
         gain = consts.tile([P, HEAD], BF16, name="gain")
         nc.sync.dma_start(out=gain[:], in_=g.partition_broadcast(P))
         bias = consts.tile([P, CHANNELS], BF16, name="bias")
-        nc.sync.dma_start(out=bias[:], in_=b.partition_broadcast(P))
-        for n in range(4, RAW_BUFS):
+
+        def load_bias(first, last):
+            columns = slice(first * BLOCK, last * BLOCK)
+            nc.sync.dma_start(out=bias[:, columns], in_=b[columns].partition_broadcast(P))
+
+        load_bias(0, 2)
+        for n in range(6, RAW_BUFS):
             load(n)
+        load_bias(2, W_BLOCKS)
 
         table = []
 
@@ -127,20 +137,30 @@ def tile_selfattention_pa_kernel(tc, x, freqs, w, b, g, out):
         def passes_of(n):
             return range((n % 2) * HALF, (n % 2 + 1) * HALF)
 
+        def spread(n):
+            if not FIRST_SPREAD <= n < PREPARATIONS:
+                return
+            first_pass = raw_tiles[n][:].bitcast(F32)[:, :, :WORDS]
+            tile = spread_pool.tile([P, 2, 2, P], F32, name="spread")
+            copy = nc.vector.tensor_copy if n % 2 == 0 else nc.scalar.copy
+            copy(out=tile[:], in_=first_pass.rearrange("p c (i u) -> p c u i", u=2))
+            spread_tiles[n] = tile
+
         def transpose(n):
             if not 0 <= n < PREPARATIONS:
                 return
             words = raw_tiles.pop(n)[:].bitcast(F32)
+            spread_tile = spread_tiles.pop(n, None)
             flipped_banks[n] = []
             for local in range(HALF):
                 flipped = flipped_psum.tile([P, 2, BLOCK], F32, name="flipped")
                 for c in range(2):
                     for u in range(2):
-                        nc.tensor.transpose(
-                            flipped[:, u, c * P : (c + 1) * P],
-                            words[:, c, local * WORDS + u : (local + 1) * WORDS : 2],
-                            ident[:],
-                        )
+                        if local == 0 and spread_tile is not None:
+                            in_ = spread_tile[:, c, u]
+                        else:
+                            in_ = words[:, c, local * WORDS + u : (local + 1) * WORDS : 2]
+                        nc.tensor.transpose(flipped[:, u, c * P : (c + 1) * P], in_, ident[:])
                 flipped_banks[n].append(flipped)
             load(n + RAW_BUFS)
 
@@ -219,11 +239,12 @@ def tile_selfattention_pa_kernel(tc, x, freqs, w, b, g, out):
         def root(n):
             if n is None:
                 return
-            rms = stats.tile([P, GROUPS], F32, name="rms")
+            inv_rms = stats.tile([P, GROUPS], F32, name="inv_rms")
             nc.scalar.activation(
-                out=rms[:], in_=square_sums.pop(n)[:], func=ACT.Sqrt, scale=1.0 / HEAD, bias=eps[:]
+                out=inv_rms[:], in_=square_sums.pop(n)[:], func=ACT.Abs_reciprocal_sqrt,
+                scale=1.0 / HEAD, bias=eps[:],
             )
-            rms_values[n] = rms
+            inverse_rms[n] = inv_rms
 
         def multiply_by_tables(n):
             if n is None:
@@ -255,13 +276,6 @@ def tile_selfattention_pa_kernel(tc, x, freqs, w, b, g, out):
             )
             rotated_tiles[n] = rotated
 
-        def invert(n):
-            if n is None:
-                return
-            inv_rms = stats.tile([P, GROUPS], F32, name="inv_rms")
-            nc.vector.reciprocal(out=inv_rms[:], in_=rms_values.pop(n)[:])
-            inverse_rms[n] = inv_rms
-
         def scale_and_store(n):
             if n is None:
                 return
@@ -285,8 +299,8 @@ def tile_selfattention_pa_kernel(tc, x, freqs, w, b, g, out):
             quantise(t - QUANTISE_LAG)
             multiply_by_tables(bank_of_step.get(t - PRODUCT_LAG))
             sum_squares(bank_of_step.get(t - PRODUCT_LAG))
+            spread(t + 1)
             add_products(bank_of_step.get(t - ADD_LAG))
-            invert(bank_of_step.get(t - ADD_LAG))
             scale_and_store(bank_of_step.get(t - STORE_LAG))
             root(bank_of_step.get(t - PRODUCT_LAG))
 

@@ -36,10 +36,10 @@ REGROUP_LAG = 1
 QUANTISE_LAG = 2
 MULTIPLY_LAG = 2 * X_BLOCKS + 2 + QUANTISE_LAG
 BIAS_LAG = 1
+SQUARE_LAG = 1
 PRODUCT_LAG = 2
 ADD_LAG = 3
-STORE_LAG = 4
-STEPS = BANKS + MULTIPLY_LAG + STORE_LAG
+STEPS = BANKS + MULTIPLY_LAG + ADD_LAG
 
 FLOPS = 2 * TOKENS * CHANNELS * CHANNELS
 
@@ -62,6 +62,7 @@ def tile_selfattention_pa_kernel(tc, x, freqs, w, b, g, out):
         w_mx = ctx.enter_context(tc.tile_pool(name="w_mx", bufs=3))
         spread_pool = ctx.enter_context(tc.tile_pool(name="spread", bufs=3))
         work = ctx.enter_context(tc.tile_pool(name="work", bufs=3))
+        out_pool = ctx.enter_context(tc.tile_pool(name="out_pool", bufs=6))
         stats = ctx.enter_context(tc.tile_pool(name="stats", bufs=4))
         flipped_psum = ctx.enter_context(tc.psum_pool(name="flipped_psum", bufs=2 * HALF))
         acc_psum = ctx.enter_context(tc.psum_pool(name="acc_psum", bufs=2))
@@ -76,7 +77,6 @@ def tile_selfattention_pa_kernel(tc, x, freqs, w, b, g, out):
         square_sums = {}
         inverse_rms = {}
         product_tiles = {}
-        rotated_tiles = {}
 
         def load(n):
             if n < PREPARATIONS:
@@ -142,8 +142,7 @@ def tile_selfattention_pa_kernel(tc, x, freqs, w, b, g, out):
                 return
             first_pass = raw_tiles[n][:].bitcast(F32)[:, :, :WORDS]
             tile = spread_pool.tile([P, 2, 2, P], F32, name="spread")
-            copy = nc.vector.tensor_copy if n % 2 == 0 else nc.scalar.copy
-            copy(out=tile[:], in_=first_pass.rearrange("p c (i u) -> p c u i", u=2))
+            nc.scalar.copy(out=tile[:], in_=first_pass.rearrange("p c (i u) -> p c u i", u=2))
             spread_tiles[n] = tile
 
         def transpose(n):
@@ -226,7 +225,7 @@ def tile_selfattention_pa_kernel(tc, x, freqs, w, b, g, out):
         def sum_squares(n):
             if n is None:
                 return
-            by_group = biased.pop(n)[:].rearrange("p c (h d) -> p (c h) d", d=HEAD)
+            by_group = biased[n][:].rearrange("p c (h d) -> p (c h) d", d=HEAD)
             squares = work.tile([P, GROUPS, HEAD], F32, name="squares")
             sums = stats.tile([P, GROUPS], F32, name="sums")
             for k in range(GROUPS):
@@ -250,45 +249,38 @@ def tile_selfattention_pa_kernel(tc, x, freqs, w, b, g, out):
             if n is None:
                 return
             xb = n % X_BLOCKS
-            shape = [P, 2, HEADS_IN_BLOCK, PAIRS, 2]
-            pairs = biased[n][:].rearrange("p c (h j i) -> p c h j i", h=HEADS_IN_BLOCK, i=2)
+            inv_rms = inverse_rms.pop(n)
+            pairs = biased.pop(n)[:].rearrange("p m (h j i) -> p (m h) j i", h=HEADS_IN_BLOCK, i=2)
             product_tiles[n] = []
             for c in range(2):
-                product = work.tile(shape, F32, name="product%d" % c)
-                nc.vector.tensor_tensor(
-                    out=product[:],
-                    in0=pairs[:, :, :, :, c : c + 1].to_broadcast(shape),
-                    in1=table[c][:, 2 * xb : 2 * xb + 2].unsqueeze(2).to_broadcast(shape),
-                    op=ALU.mult,
-                )
+                product = work.tile([P, GROUPS, PAIRS, 2], F32, name="product%d" % c)
+                for k in range(GROUPS):
+                    nc.vector.scalar_tensor_tensor(
+                        out=product[:, k],
+                        in0=pairs[:, k, :, c : c + 1].to_broadcast([P, PAIRS, 2]),
+                        scalar=inv_rms[:, k : k + 1],
+                        in1=table[c][:, 2 * xb + k // HEADS_IN_BLOCK],
+                        op0=ALU.mult,
+                        op1=ALU.mult,
+                    )
                 product_tiles[n].append(product)
 
-        def add_products(n):
+        def add_and_store(n):
             if n is None:
                 return
+            xb = n % X_BLOCKS
             first, second = product_tiles.pop(n)
-            rotated = work.tile([P, GROUPS, HEAD], F32, name="rotated")
+            rotated = out_pool.tile([P, GROUPS, HEAD], F32, name="rotated")
             nc.vector.tensor_tensor(
                 out=rotated[:].rearrange("p k d -> p (k d)"),
-                in0=first[:].rearrange("p c h j i -> p (c h j i)"),
-                in1=second[:].rearrange("p c h j i -> p (c h j i)"),
+                in0=first[:].rearrange("p k j i -> p (k j i)"),
+                in1=second[:].rearrange("p k j i -> p (k j i)"),
                 op=ALU.add,
             )
-            rotated_tiles[n] = rotated
-
-        def scale_and_store(n):
-            if n is None:
-                return
-            xb, wb = n % X_BLOCKS, n // X_BLOCKS
-            rotated, inv_rms = rotated_tiles.pop(n), inverse_rms.pop(n)
-            result = work.tile([P, GROUPS, HEAD], F32, name="result")
-            for k in range(GROUPS):
-                nc.scalar.activation(
-                    out=result[:, k, :], in_=rotated[:, k, :], func=ACT.Copy, scale=inv_rms[:, k : k + 1]
-                )
+            wb = n // X_BLOCKS
             nc.sync.dma_start(
                 out=out_view[:, 2 * xb : 2 * xb + 2, wb * BLOCK : (wb + 1) * BLOCK],
-                in_=result[:].rearrange("p (c h) d -> p c (h d)", c=2),
+                in_=rotated[:].rearrange("p (m h) d -> p m (h d)", m=2),
             )
 
         def step(t):
@@ -297,12 +289,11 @@ def tile_selfattention_pa_kernel(tc, x, freqs, w, b, g, out):
             multiply(bank_of_step.get(t))
             transpose(t)
             quantise(t - QUANTISE_LAG)
-            multiply_by_tables(bank_of_step.get(t - PRODUCT_LAG))
-            sum_squares(bank_of_step.get(t - PRODUCT_LAG))
+            sum_squares(bank_of_step.get(t - SQUARE_LAG))
             spread(t + 1)
-            add_products(bank_of_step.get(t - ADD_LAG))
-            scale_and_store(bank_of_step.get(t - STORE_LAG))
-            root(bank_of_step.get(t - PRODUCT_LAG))
+            root(bank_of_step.get(t - SQUARE_LAG))
+            multiply_by_tables(bank_of_step.get(t - PRODUCT_LAG))
+            add_and_store(bank_of_step.get(t - ADD_LAG))
 
         first_multiply = min(bank_of_step)
         for t in range(first_multiply):

@@ -21,25 +21,24 @@ EPS = 1e-6
 K_PASS = 4 * P
 PASSES = CHANNELS // K_PASS
 WORDS = K_PASS // 2
-BLOCK = 2 * P
-X_BLOCKS = TOKENS // BLOCK
+HALF = PASSES // 2
+BLOCK = 2 * HEAD
 W_BLOCKS = CHANNELS // BLOCK
 HEADS_IN_BLOCK = BLOCK // HEAD
-HALF = PASSES // 2
-FIRST_SPREAD = 4
-RAW_BUFS = 12
-PREPARATIONS = 2 * (X_BLOCKS + W_BLOCKS)
-BANKS = X_BLOCKS * W_BLOCKS
+X_PAIRS = TOKENS // (2 * P)
+BANKS = X_PAIRS * W_BLOCKS
 GROUPS = 2 * HEADS_IN_BLOCK
 
-REGROUP_LAG = 1
-QUANTISE_LAG = 2
-MULTIPLY_LAG = 2 * X_BLOCKS + 2 + QUANTISE_LAG
-BIAS_LAG = 1
+UNIT_BANKS = 3
+RAW_BUFS = 12
+FIRST_SPREAD = 8
+CONSTANTS_AFTER = 5
+
+QUANTISE_LAG = 1
 SQUARE_LAG = 1
 PRODUCT_LAG = 2
 ADD_LAG = 3
-STEPS = BANKS + MULTIPLY_LAG + ADD_LAG
+MULTIPLY_LAG = 7
 
 FLOPS = 2 * TOKENS * CHANNELS * CHANNELS
 
@@ -50,21 +49,28 @@ def tile_selfattention_pa_kernel(tc, x, freqs, w, b, g, out):
     freqs_view = freqs.rearrange("o (m p) q j i c -> p (o m q) (j i c)", p=P)
     out_view = out.rearrange("o (m p) h d -> p (o m) (h d)", p=P)
 
-    blocks = [("x", 0), ("w", 0), ("x", 1)] + [("w", i) for i in range(1, W_BLOCKS)]
-    bank_of_step = {n + MULTIPLY_LAG - max(0, 2 - n): n for n in range(BANKS)}
+    units = [("x", 0, 0), ("w", 0, 0), ("w", 0, 1), ("x", 1, 0), ("x", 2, 0), ("x", 3, 0)]
+    units += [("w", i, half) for i in range(1, W_BLOCKS) for half in range(2)]
+
+    piece_of_step = {4: (0, 0, 1), 5: (0, 1, 1), 6: (1, 0, 1), 7: (1, 1, 1)}
+    piece_of_step.update({n + MULTIPLY_LAG: (n, 0, 2) for n in range(2, BANKS - 1)})
+    last = BANKS - 1
+    piece_of_step.update({last + MULTIPLY_LAG: (last, 0, 1), last + MULTIPLY_LAG + 1: (last, 1, 1)})
+    first_piece = min(piece_of_step)
+    last_piece = max(piece_of_step)
 
     with ExitStack() as ctx:
         ctx.enter_context(tc.manual_schedule())
         consts = ctx.enter_context(tc.tile_pool(name="consts", bufs=1))
         raw_pool = ctx.enter_context(tc.tile_pool(name="raw", bufs=RAW_BUFS))
-        grouped_pool = ctx.enter_context(tc.tile_pool(name="grouped", bufs=3 * HALF))
+        spread_pool = ctx.enter_context(tc.tile_pool(name="spread", bufs=3))
+        grouped_pool = ctx.enter_context(tc.tile_pool(name="grouped", bufs=3 * UNIT_BANKS))
         x_mx = ctx.enter_context(tc.tile_pool(name="x_mx", bufs=1))
         w_mx = ctx.enter_context(tc.tile_pool(name="w_mx", bufs=3))
-        spread_pool = ctx.enter_context(tc.tile_pool(name="spread", bufs=3))
         work = ctx.enter_context(tc.tile_pool(name="work", bufs=3))
-        out_pool = ctx.enter_context(tc.tile_pool(name="out_pool", bufs=6))
         stats = ctx.enter_context(tc.tile_pool(name="stats", bufs=4))
-        flipped_psum = ctx.enter_context(tc.psum_pool(name="flipped_psum", bufs=2 * HALF))
+        results = ctx.enter_context(tc.tile_pool(name="results", bufs=8))
+        flipped_psum = ctx.enter_context(tc.psum_pool(name="flipped_psum", bufs=2 * UNIT_BANKS))
         acc_psum = ctx.enter_context(tc.psum_pool(name="acc_psum", bufs=2))
 
         raw_tiles = {}
@@ -79,20 +85,26 @@ def tile_selfattention_pa_kernel(tc, x, freqs, w, b, g, out):
         product_tiles = {}
 
         def load(n):
-            if n < PREPARATIONS:
-                kind, i = blocks[n // 2]
-                rows = (x_rows if kind == "x" else w)[i * BLOCK : (i + 1) * BLOCK, :]
-                first = (n % 2) * HALF * K_PASS
-                raw = raw_pool.tile([P, 2, HALF * K_PASS], BF16, name="raw")
-                width = K_PASS if n == 0 else HALF * K_PASS
-                for k in range(0, HALF * K_PASS, width):
+            if n >= len(units):
+                return
+            kind, i, half = units[n]
+            if kind == "x":
+                raw = raw_pool.tile([P, 1, CHANNELS], BF16, name="raw")
+                width = CHANNELS // 3 if n == 0 else CHANNELS
+                for k in range(0, CHANNELS, width):
                     nc.sync.dma_start(
-                        out=raw[:, :, k : k + width],
-                        in_=rows[:, first + k : first + k + width].rearrange("(c p) k -> p c k", p=P),
+                        out=raw[:, 0, k : k + width], in_=x_rows[i * P : (i + 1) * P, k : k + width]
                     )
-                raw_tiles[n] = raw
+            else:
+                raw = raw_pool.tile([P, 2, HALF * K_PASS], BF16, name="raw")
+                columns = slice(half * HALF * K_PASS, (half + 1) * HALF * K_PASS)
+                nc.sync.dma_start(
+                    out=raw[:],
+                    in_=w[i * BLOCK : (i + 1) * BLOCK, columns].rearrange("(c p) k -> p c k", p=P),
+                )
+            raw_tiles[n] = raw
 
-        for n in range(6):
+        for n in range(CONSTANTS_AFTER):
             load(n)
 
         eps = consts.tile([P, 1], F32, name="eps")
@@ -108,12 +120,12 @@ def tile_selfattention_pa_kernel(tc, x, freqs, w, b, g, out):
         nc.sync.dma_start(out=gain[:], in_=g.partition_broadcast(P))
         bias = consts.tile([P, CHANNELS], BF16, name="bias")
 
-        def load_bias(first, last):
-            columns = slice(first * BLOCK, last * BLOCK)
+        def load_bias(first, end):
+            columns = slice(first * BLOCK, end * BLOCK)
             nc.sync.dma_start(out=bias[:, columns], in_=b[columns].partition_broadcast(P))
 
         load_bias(0, 2)
-        for n in range(6, RAW_BUFS):
+        for n in range(CONSTANTS_AFTER, RAW_BUFS):
             load(n)
         load_bias(2, W_BLOCKS)
 
@@ -134,11 +146,8 @@ def tile_selfattention_pa_kernel(tc, x, freqs, w, b, g, out):
                 )
                 table.append(tab)
 
-        def passes_of(n):
-            return range((n % 2) * HALF, (n % 2 + 1) * HALF)
-
         def spread(n):
-            if not FIRST_SPREAD <= n < PREPARATIONS:
+            if not FIRST_SPREAD <= n < len(units):
                 return
             first_pass = raw_tiles[n][:].bitcast(F32)[:, :, :WORDS]
             tile = spread_pool.tile([P, 2, 2, P], F32, name="spread")
@@ -146,158 +155,162 @@ def tile_selfattention_pa_kernel(tc, x, freqs, w, b, g, out):
             spread_tiles[n] = tile
 
         def transpose(n):
-            if not 0 <= n < PREPARATIONS:
+            if n >= len(units):
                 return
+            kind = units[n][0]
             words = raw_tiles.pop(n)[:].bitcast(F32)
             spread_tile = spread_tiles.pop(n, None)
             flipped_banks[n] = []
-            for local in range(HALF):
-                flipped = flipped_psum.tile([P, 2, BLOCK], F32, name="flipped")
-                for c in range(2):
+            for bank in range(UNIT_BANKS):
+                flipped = flipped_psum.tile([P, 2, 2, P], F32, name="flipped")
+                for s in range(2):
+                    c, q = (0, 2 * bank + s) if kind == "x" else (s, bank)
                     for u in range(2):
-                        if local == 0 and spread_tile is not None:
+                        if q == 0 and spread_tile is not None:
                             in_ = spread_tile[:, c, u]
                         else:
-                            in_ = words[:, c, local * WORDS + u : (local + 1) * WORDS : 2]
-                        nc.tensor.transpose(flipped[:, u, c * P : (c + 1) * P], in_, ident[:])
+                            in_ = words[:, c, q * WORDS + u : (q + 1) * WORDS : 2]
+                        nc.tensor.transpose(flipped[:, s, u], in_, ident[:])
                 flipped_banks[n].append(flipped)
             load(n + RAW_BUFS)
 
         def regroup(n):
-            if not 0 <= n < PREPARATIONS:
+            if n >= len(units):
                 return
             grouped_tiles[n] = []
             for flipped in flipped_banks.pop(n):
                 grouped = grouped_pool.tile([P, 4 * BLOCK], BF16, name="grouped", align_bytes=64)
                 nc.scalar.copy(
-                    out=grouped[:].bitcast(F32).rearrange("p (r u) -> p r u", u=2),
-                    in_=flipped[:].rearrange("p u r -> p r u"),
+                    out=grouped[:].bitcast(F32).rearrange("p (a r u) -> p a r u", a=2, u=2),
+                    in_=flipped[:].rearrange("p a u r -> p a r u"),
                 )
                 grouped_tiles[n].append(grouped)
 
         def quantise(n):
-            if not 0 <= n < PREPARATIONS:
+            if not 0 <= n < len(units):
                 return
-            block = blocks[n // 2]
-            if n % 2 == 0:
-                pool, name = (x_mx, "x%d" % block[1]) if block[0] == "x" else (w_mx, "w")
-                codes = pool.tile([P, PASSES, BLOCK], U32, name=name + "_codes", align_bytes=64)
-                scales = pool.tile([P, PASSES, BLOCK], U8, name=name + "_scales", align_bytes=64)
-                mx_operands[block] = (codes, scales)
-            codes, scales = mx_operands[block]
-            for q, grouped in zip(passes_of(n), grouped_tiles.pop(n)):
+            kind, i, half = units[n]
+            if half == 0:
+                pool, name, rows = (x_mx, "x%d" % i, P) if kind == "x" else (w_mx, "w", BLOCK)
+                codes = pool.tile([P, PASSES, rows], U32, name=name + "_codes", align_bytes=64)
+                scales = pool.tile([P, PASSES, rows], U8, name=name + "_scales", align_bytes=64)
+                mx_operands[kind, i] = (codes, scales)
+            codes, scales = mx_operands[kind, i]
+            codes_row = codes[:].rearrange("p q r -> p (q r)")
+            scales_row = scales[:].rearrange("p q r -> p (q r)")
+            for bank, grouped in enumerate(grouped_tiles.pop(n)):
+                first = (half * UNIT_BANKS + bank) * BLOCK
                 nc.vector.quantize_mx(
-                    out=codes[:, q, :].bitcast(FP8X4), scales=scales[:, q, :], in_=grouped[:]
+                    out=codes_row[:, first : first + BLOCK].bitcast(FP8X4),
+                    scales=scales_row[:, first : first + BLOCK],
+                    in_=grouped[:],
                 )
 
-        def multiply(n):
-            if n is None:
+        def multiply(piece):
+            if piece is None:
                 return
-            x_codes, x_scales = mx_operands[("x", n % X_BLOCKS)]
-            w_codes, w_scales = mx_operands[("w", n // X_BLOCKS)]
-            acc = acc_psum.tile([P, 2, BLOCK], F32, name="acc")
-            for c in range(2):
+            n, m, count = piece
+            w_codes, w_scales = mx_operands["w", n // X_PAIRS]
+            if m == 0:
+                acc = acc_psum.tile([P, 2, BLOCK], F32, name="acc")
+                acc_banks[n] = acc
+            for c in range(m, m + count):
+                x_codes, x_scales = mx_operands["x", 2 * (n % X_PAIRS) + c]
                 for q in range(PASSES):
                     nc.tensor.matmul_mx(
-                        out=acc[:, c, :],
-                        lhsT=x_codes[:, q, c * P : (c + 1) * P].bitcast(FP8X4),
-                        lhsT_scale=x_scales[:, q, c * P : (c + 1) * P],
+                        out=acc_banks[n][:, c, :],
+                        lhsT=x_codes[:, q, :].bitcast(FP8X4),
+                        lhsT_scale=x_scales[:, q, :],
                         rhs=w_codes[:, q, :].bitcast(FP8X4),
                         rhs_scale=w_scales[:, q, :],
                         start=(q == 0),
                         stop=(q == PASSES - 1),
                     )
-            acc_banks[n] = acc
 
-        def add_bias(n):
-            if n is None:
+        def add_bias(piece):
+            if piece is None:
                 return
-            wb = n // X_BLOCKS
+            n, m, count = piece
+            block = n // X_PAIRS
             u = work.tile([P, 2, BLOCK], F32, name="u")
             nc.vector.tensor_tensor(
-                out=u[:],
-                in0=acc_banks.pop(n)[:],
-                in1=bias[:, wb * BLOCK : (wb + 1) * BLOCK].unsqueeze(1).to_broadcast([P, 2, BLOCK]),
+                out=u[:, :count, :],
+                in0=acc_banks[n][:, m : m + count, :],
+                in1=bias[:, block * BLOCK : (block + 1) * BLOCK]
+                .unsqueeze(1)
+                .to_broadcast([P, count, BLOCK]),
                 op=ALU.add,
             )
-            biased[n] = u
+            biased[piece] = u
 
-        def sum_squares(n):
-            if n is None:
+        def invert_rms(piece):
+            if piece is None:
                 return
-            by_group = biased[n][:].rearrange("p c (h d) -> p (c h) d", d=HEAD)
+            groups = piece[2] * HEADS_IN_BLOCK
+            by_group = biased[piece][:].rearrange("p m (h d) -> p (m h) d", d=HEAD)
             squares = work.tile([P, GROUPS, HEAD], F32, name="squares")
             sums = stats.tile([P, GROUPS], F32, name="sums")
-            for k in range(GROUPS):
+            inv_rms = stats.tile([P, GROUPS], F32, name="inv_rms")
+            for k in range(groups):
                 nc.scalar.activation(
                     out=squares[:, k, :], in_=by_group[:, k, :], func=ACT.Square,
                     accum_out=sums[:, k : k + 1],
                 )
-            square_sums[n] = sums
-
-        def root(n):
-            if n is None:
-                return
-            inv_rms = stats.tile([P, GROUPS], F32, name="inv_rms")
             nc.scalar.activation(
-                out=inv_rms[:], in_=square_sums.pop(n)[:], func=ACT.Abs_reciprocal_sqrt,
+                out=inv_rms[:, :groups], in_=sums[:, :groups], func=ACT.Abs_reciprocal_sqrt,
                 scale=1.0 / HEAD, bias=eps[:],
             )
-            inverse_rms[n] = inv_rms
+            inverse_rms[piece] = inv_rms
 
-        def multiply_by_tables(n):
-            if n is None:
+        def multiply_by_tables(piece):
+            if piece is None:
                 return
-            xb = n % X_BLOCKS
-            inv_rms = inverse_rms.pop(n)
-            pairs = biased.pop(n)[:].rearrange("p m (h j i) -> p (m h) j i", h=HEADS_IN_BLOCK, i=2)
-            product_tiles[n] = []
+            n, m, count = piece
+            inv_rms = inverse_rms.pop(piece)
+            pairs = biased.pop(piece)[:].rearrange("p m (h j i) -> p (m h) j i", h=HEADS_IN_BLOCK, i=2)
+            product_tiles[piece] = []
             for c in range(2):
                 product = work.tile([P, GROUPS, PAIRS, 2], F32, name="product%d" % c)
-                for k in range(GROUPS):
+                for k in range(count * HEADS_IN_BLOCK):
+                    token_tile = 2 * (n % X_PAIRS) + m + k // HEADS_IN_BLOCK
                     nc.vector.scalar_tensor_tensor(
                         out=product[:, k],
                         in0=pairs[:, k, :, c : c + 1].to_broadcast([P, PAIRS, 2]),
                         scalar=inv_rms[:, k : k + 1],
-                        in1=table[c][:, 2 * xb + k // HEADS_IN_BLOCK],
+                        in1=table[c][:, token_tile],
                         op0=ALU.mult,
                         op1=ALU.mult,
                     )
-                product_tiles[n].append(product)
+                product_tiles[piece].append(product)
 
-        def add_and_store(n):
-            if n is None:
+        def add_and_store(piece):
+            if piece is None:
                 return
-            xb = n % X_BLOCKS
-            first, second = product_tiles.pop(n)
-            rotated = out_pool.tile([P, GROUPS, HEAD], F32, name="rotated")
+            n, m, count = piece
+            groups = count * HEADS_IN_BLOCK
+            first, second = product_tiles.pop(piece)
+            rotated = results.tile([P, GROUPS, HEAD], F32, name="rotated")
             nc.vector.tensor_tensor(
-                out=rotated[:].rearrange("p k d -> p (k d)"),
-                in0=first[:].rearrange("p k j i -> p (k j i)"),
-                in1=second[:].rearrange("p k j i -> p (k j i)"),
+                out=rotated[:, :groups].rearrange("p k d -> p (k d)"),
+                in0=first[:, :groups].rearrange("p k j i -> p (k j i)"),
+                in1=second[:, :groups].rearrange("p k j i -> p (k j i)"),
                 op=ALU.add,
             )
-            wb = n // X_BLOCKS
+            token_tile, block = 2 * (n % X_PAIRS) + m, n // X_PAIRS
             nc.sync.dma_start(
-                out=out_view[:, 2 * xb : 2 * xb + 2, wb * BLOCK : (wb + 1) * BLOCK],
-                in_=rotated[:].rearrange("p (m h) d -> p m (h d)", m=2),
+                out=out_view[:, token_tile : token_tile + count, block * BLOCK : (block + 1) * BLOCK],
+                in_=rotated[:, :groups].rearrange("p (m h) d -> p m (h d)", h=HEADS_IN_BLOCK),
             )
 
-        def step(t):
-            add_bias(bank_of_step.get(t - BIAS_LAG))
-            regroup(t - REGROUP_LAG)
-            multiply(bank_of_step.get(t))
+        for t in range(last_piece + ADD_LAG + 1):
+            multiply(piece_of_step.get(t))
             transpose(t)
-            quantise(t - QUANTISE_LAG)
-            sum_squares(bank_of_step.get(t - SQUARE_LAG))
+            invert_rms(piece_of_step.get(t - SQUARE_LAG))
+            multiply_by_tables(piece_of_step.get(t - PRODUCT_LAG))
+            add_and_store(piece_of_step.get(t - ADD_LAG))
             spread(t + 1)
-            root(bank_of_step.get(t - SQUARE_LAG))
-            multiply_by_tables(bank_of_step.get(t - PRODUCT_LAG))
-            add_and_store(bank_of_step.get(t - ADD_LAG))
-
-        first_multiply = min(bank_of_step)
-        for t in range(first_multiply):
-            step(t)
-        build_tables()
-        for t in range(first_multiply, STEPS):
-            step(t)
+            quantise(t - QUANTISE_LAG)
+            add_bias(piece_of_step.get(t))
+            if t == first_piece + PRODUCT_LAG - 1:
+                build_tables()
+            regroup(t)

@@ -146,13 +146,16 @@ def tile_selfattention_pa_kernel(tc, x, freqs, w, b, g, out):
                 )
                 table.append(tab)
 
-        def spread(n):
+        def spread(n, c):
             if not FIRST_SPREAD <= n < len(units):
                 return
             first_pass = raw_tiles[n][:].bitcast(F32)[:, :, :WORDS]
-            tile = spread_pool.tile([P, 2, 2, P], F32, name="spread")
-            nc.scalar.copy(out=tile[:], in_=first_pass.rearrange("p c (i u) -> p c u i", u=2))
-            spread_tiles[n] = tile
+            if c == 0:
+                tile = spread_pool.tile([P, 2, 2, P], F32, name="spread")
+                spread_tiles[n] = tile
+            nc.scalar.copy(
+                out=spread_tiles[n][:, c], in_=first_pass[:, c].rearrange("p (i u) -> p u i", u=2)
+            )
 
         def transpose(n):
             if n >= len(units):
@@ -243,22 +246,27 @@ def tile_selfattention_pa_kernel(tc, x, freqs, w, b, g, out):
             )
             biased[piece] = u
 
-        def invert_rms(piece):
+        def sum_squares(piece):
             if piece is None:
                 return
-            groups = piece[2] * HEADS_IN_BLOCK
             by_group = biased[piece][:].rearrange("p m (h d) -> p (m h) d", d=HEAD)
             squares = work.tile([P, GROUPS, HEAD], F32, name="squares")
             sums = stats.tile([P, GROUPS], F32, name="sums")
-            inv_rms = stats.tile([P, GROUPS], F32, name="inv_rms")
-            for k in range(groups):
+            for k in range(piece[2] * HEADS_IN_BLOCK):
                 nc.scalar.activation(
                     out=squares[:, k, :], in_=by_group[:, k, :], func=ACT.Square,
                     accum_out=sums[:, k : k + 1],
                 )
+            square_sums[piece] = sums
+
+        def invert_rms(piece):
+            if piece is None:
+                return
+            groups = piece[2] * HEADS_IN_BLOCK
+            inv_rms = stats.tile([P, GROUPS], F32, name="inv_rms")
             nc.scalar.activation(
-                out=inv_rms[:, :groups], in_=sums[:, :groups], func=ACT.Abs_reciprocal_sqrt,
-                scale=1.0 / HEAD, bias=eps[:],
+                out=inv_rms[:, :groups], in_=square_sums.pop(piece)[:, :groups],
+                func=ACT.Abs_reciprocal_sqrt, scale=1.0 / HEAD, bias=eps[:],
             )
             inverse_rms[piece] = inv_rms
 
@@ -305,10 +313,12 @@ def tile_selfattention_pa_kernel(tc, x, freqs, w, b, g, out):
         for t in range(last_piece + ADD_LAG + 1):
             multiply(piece_of_step.get(t))
             transpose(t)
-            invert_rms(piece_of_step.get(t - SQUARE_LAG))
+            sum_squares(piece_of_step.get(t - SQUARE_LAG))
             multiply_by_tables(piece_of_step.get(t - PRODUCT_LAG))
             add_and_store(piece_of_step.get(t - ADD_LAG))
-            spread(t + 1)
+            spread(t + 1, 0)
+            invert_rms(piece_of_step.get(t - SQUARE_LAG))
+            spread(t + 1, 1)
             quantise(t - QUANTISE_LAG)
             add_bias(piece_of_step.get(t))
             if t == first_piece + PRODUCT_LAG - 1:

@@ -30,6 +30,7 @@ BANKS = X_PAIRS * W_BLOCKS
 GROUPS = 2 * HEADS_IN_BLOCK
 
 UNIT_BANKS = 3
+SPREAD_PARTS = ((0, 0), (0, 1), (1, 0))
 RAW_BUFS = 12
 FIRST_SPREAD = 8
 CONSTANTS_AFTER = 5
@@ -63,7 +64,7 @@ def tile_selfattention_pa_kernel(tc, x, freqs, w, b, g, out):
         ctx.enter_context(tc.manual_schedule())
         consts = ctx.enter_context(tc.tile_pool(name="consts", bufs=1))
         raw_pool = ctx.enter_context(tc.tile_pool(name="raw", bufs=RAW_BUFS))
-        spread_pool = ctx.enter_context(tc.tile_pool(name="spread", bufs=3))
+        spread_pool = ctx.enter_context(tc.tile_pool(name="spread", bufs=9))
         grouped_pool = ctx.enter_context(tc.tile_pool(name="grouped", bufs=3 * UNIT_BANKS))
         x_mx = ctx.enter_context(tc.tile_pool(name="x_mx", bufs=1))
         w_mx = ctx.enter_context(tc.tile_pool(name="w_mx", bufs=3))
@@ -146,31 +147,30 @@ def tile_selfattention_pa_kernel(tc, x, freqs, w, b, g, out):
                 )
                 table.append(tab)
 
-        def spread(n, c):
+        def spread(n, part):
             if not FIRST_SPREAD <= n < len(units):
                 return
-            first_pass = raw_tiles[n][:].bitcast(F32)[:, :, :WORDS]
-            if c == 0:
-                tile = spread_pool.tile([P, 2, 2, P], F32, name="spread")
-                spread_tiles[n] = tile
-            nc.scalar.copy(
-                out=spread_tiles[n][:, c], in_=first_pass[:, c].rearrange("p (i u) -> p u i", u=2)
-            )
+            if part == 2 and n % 2 == 1:
+                return
+            q, c = SPREAD_PARTS[part]
+            rows = raw_tiles[n][:].bitcast(F32)[:, c, q * WORDS : (q + 1) * WORDS]
+            tile = spread_pool.tile([P, 2, P], F32, name="spread")
+            nc.scalar.copy(out=tile[:], in_=rows.rearrange("p (i u) -> p u i", u=2))
+            spread_tiles[n, q, c] = tile
 
         def transpose(n):
             if n >= len(units):
                 return
             kind = units[n][0]
             words = raw_tiles.pop(n)[:].bitcast(F32)
-            spread_tile = spread_tiles.pop(n, None)
             flipped_banks[n] = []
             for bank in range(UNIT_BANKS):
                 flipped = flipped_psum.tile([P, 2, 2, P], F32, name="flipped")
                 for s in range(2):
                     c, q = (0, 2 * bank + s) if kind == "x" else (s, bank)
                     for u in range(2):
-                        if q == 0 and spread_tile is not None:
-                            in_ = spread_tile[:, c, u]
+                        if (n, q, c) in spread_tiles:
+                            in_ = spread_tiles[n, q, c][:, u]
                         else:
                             in_ = words[:, c, q * WORDS + u : (q + 1) * WORDS : 2]
                         nc.tensor.transpose(flipped[:, s, u], in_, ident[:])
@@ -318,7 +318,8 @@ def tile_selfattention_pa_kernel(tc, x, freqs, w, b, g, out):
             add_and_store(piece_of_step.get(t - ADD_LAG))
             spread(t + 1, 0)
             invert_rms(piece_of_step.get(t - SQUARE_LAG))
-            spread(t + 1, 1)
+            for part in range(1, len(SPREAD_PARTS)):
+                spread(t + 1, part)
             quantise(t - QUANTISE_LAG)
             add_bias(piece_of_step.get(t))
             if t == first_piece + PRODUCT_LAG - 1:

from contextlib import ExitStack

import concourse.mybir as mybir
from concourse.masks import make_identity

F32 = mybir.dt.float32
BF16 = mybir.dt.bfloat16
U32 = mybir.dt.uint32
U8 = mybir.dt.uint8
FP8X4 = mybir.dt.float8_e4m3fn_x4
ACT = mybir.ActivationFunctionType
ALU = mybir.AluOpType

P = 128
TOKENS = 512
CHANNELS = 3072
HEAD = 128
PAIRS = HEAD // 2
EPS = 1e-6

K_PASS = 4 * P
PASSES = CHANNELS // K_PASS
WORDS = K_PASS // 2
HALF = PASSES // 2
BLOCK = 2 * HEAD
W_BLOCKS = CHANNELS // BLOCK
HEADS_IN_BLOCK = BLOCK // HEAD
X_PAIRS = TOKENS // (2 * P)
BANKS = X_PAIRS * W_BLOCKS
GROUPS = 2 * HEADS_IN_BLOCK

UNIT_BANKS = 3
SPREAD_PARTS = ((0, 0), (0, 1), (1, 0))
RAW_BUFS = 12
FIRST_SPREAD = 8
CONSTANTS_AFTER = 5

QUANTISE_LAG = 1
SQUARE_LAG = 1
PRODUCT_LAG = 2
ADD_LAG = 3
MULTIPLY_LAG = 7

FLOPS = 2 * TOKENS * CHANNELS * CHANNELS


def tile_selfattention_pa_kernel(tc, x, freqs, w, b, g, out):
    nc = tc.nc
    x_rows = x.rearrange("o s k -> (o s) k")
    freqs_view = freqs.rearrange("o (m p) q j i c -> p (o m q) (j i c)", p=P)
    out_view = out.rearrange("o (m p) h d -> p (o m) (h d)", p=P)

    units = [("x", 0, 0), ("w", 0, 0), ("w", 0, 1), ("x", 1, 0), ("x", 2, 0), ("x", 3, 0)]
    units += [("w", i, half) for i in range(1, W_BLOCKS) for half in range(2)]

    piece_of_step = {4: (0, 0, 1), 5: (0, 1, 1), 6: (1, 0, 1), 7: (1, 1, 1)}
    piece_of_step.update({n + MULTIPLY_LAG: (n, 0, 2) for n in range(2, BANKS - 1)})
    last = BANKS - 1
    piece_of_step.update({last + MULTIPLY_LAG: (last, 0, 1), last + MULTIPLY_LAG + 1: (last, 1, 1)})
    first_piece = min(piece_of_step)
    last_piece = max(piece_of_step)

    with ExitStack() as ctx:
        ctx.enter_context(tc.manual_schedule())
        consts = ctx.enter_context(tc.tile_pool(name="consts", bufs=1))
        raw_pool = ctx.enter_context(tc.tile_pool(name="raw", bufs=RAW_BUFS))
        spread_pool = ctx.enter_context(tc.tile_pool(name="spread", bufs=9))
        grouped_pool = ctx.enter_context(tc.tile_pool(name="grouped", bufs=3 * UNIT_BANKS))
        x_mx = ctx.enter_context(tc.tile_pool(name="x_mx", bufs=1))
        w_mx = ctx.enter_context(tc.tile_pool(name="w_mx", bufs=3))
        work = ctx.enter_context(tc.tile_pool(name="work", bufs=3))
        stats = ctx.enter_context(tc.tile_pool(name="stats", bufs=4))
        results = ctx.enter_context(tc.tile_pool(name="results", bufs=8))
        flipped_psum = ctx.enter_context(tc.psum_pool(name="flipped_psum", bufs=2 * UNIT_BANKS))
        acc_psum = ctx.enter_context(tc.psum_pool(name="acc_psum", bufs=2))

        raw_tiles = {}
        spread_tiles = {}
        flipped_banks = {}
        grouped_tiles = {}
        mx_operands = {}
        acc_banks = {}
        biased = {}
        square_sums = {}
        inverse_rms = {}
        product_tiles = {}

        def load(n):
            if n >= len(units):
                return
            kind, i, half = units[n]
            if kind == "x":
                raw = raw_pool.tile([P, 1, CHANNELS], BF16, name="raw")
                width = CHANNELS // 3 if n == 0 else CHANNELS
                for k in range(0, CHANNELS, width):
                    nc.sync.dma_start(
                        out=raw[:, 0, k : k + width], in_=x_rows[i * P : (i + 1) * P, k : k + width]
                    )
            else:
                raw = raw_pool.tile([P, 2, HALF * K_PASS], BF16, name="raw")
                columns = slice(half * HALF * K_PASS, (half + 1) * HALF * K_PASS)
                nc.sync.dma_start(
                    out=raw[:],
                    in_=w[i * BLOCK : (i + 1) * BLOCK, columns].rearrange("(c p) k -> p c k", p=P),
                )
            raw_tiles[n] = raw

        for n in range(CONSTANTS_AFTER):
            load(n)

        eps = consts.tile([P, 1], F32, name="eps")
        nc.vector.memset(eps[:], EPS)
        warm = consts.tile([P, 1], F32, name="warm")
        nc.scalar.activation(out=warm[:], in_=eps[:], func=ACT.Abs_reciprocal_sqrt)
        ident = consts.tile([P, P], F32, name="ident")
        make_identity(nc, ident[:])

        freqs_sb = consts.tile([P, TOKENS // P, 4 * PAIRS], BF16, name="freqs_sb")
        nc.sync.dma_start(out=freqs_sb[:], in_=freqs_view)
        gain = consts.tile([P, HEAD], BF16, name="gain")
        nc.sync.dma_start(out=gain[:], in_=g.partition_broadcast(P))
        bias = consts.tile([P, CHANNELS], BF16, name="bias")

        def load_bias(first, end):
            columns = slice(first * BLOCK, end * BLOCK)
            nc.sync.dma_start(out=bias[:, columns], in_=b[columns].partition_broadcast(P))

        load_bias(0, 2)
        for n in range(CONSTANTS_AFTER, RAW_BUFS):
            load(n)
        load_bias(2, W_BLOCKS)

        table = []

        def build_tables():
            for c in range(2):
                tab = consts.tile([P, TOKENS // P, PAIRS, 2], F32, name="table%d" % c)
                nc.vector.tensor_tensor(
                    out=tab[:],
                    in0=freqs_sb[:].rearrange("p m (j i c) -> p c m j i", i=2, c=2)[:, c],
                    in1=gain[:]
                    .rearrange("p (j c) -> p c j", c=2)[:, c]
                    .unsqueeze(1)
                    .unsqueeze(3)
                    .to_broadcast([P, TOKENS // P, PAIRS, 2]),
                    op=ALU.mult,
                )
                table.append(tab)

        def spread(n, part):
            if not FIRST_SPREAD <= n < len(units):
                return
            if part == 2 and n % 2 == 1:
                return
            q, c = SPREAD_PARTS[part]
            rows = raw_tiles[n][:].bitcast(F32)[:, c, q * WORDS : (q + 1) * WORDS]
            tile = spread_pool.tile([P, 2, P], F32, name="spread")
            nc.scalar.copy(out=tile[:], in_=rows.rearrange("p (i u) -> p u i", u=2))
            spread_tiles[n, q, c] = tile

        def transpose(n):
            if n >= len(units):
                return
            kind = units[n][0]
            words = raw_tiles.pop(n)[:].bitcast(F32)
            flipped_banks[n] = []
            for bank in range(UNIT_BANKS):
                flipped = flipped_psum.tile([P, 2, 2, P], F32, name="flipped")
                for s in range(2):
                    c, q = (0, 2 * bank + s) if kind == "x" else (s, bank)
                    for u in range(2):
                        if (n, q, c) in spread_tiles:
                            in_ = spread_tiles[n, q, c][:, u]
                        else:
                            in_ = words[:, c, q * WORDS + u : (q + 1) * WORDS : 2]
                        nc.tensor.transpose(flipped[:, s, u], in_, ident[:])
                flipped_banks[n].append(flipped)
            load(n + RAW_BUFS)

        def regroup(n):
            if n >= len(units):
                return
            grouped_tiles[n] = []
            for flipped in flipped_banks.pop(n):
                grouped = grouped_pool.tile([P, 4 * BLOCK], BF16, name="grouped", align_bytes=64)
                nc.scalar.copy(
                    out=grouped[:].bitcast(F32).rearrange("p (a r u) -> p a r u", a=2, u=2),
                    in_=flipped[:].rearrange("p a u r -> p a r u"),
                )
                grouped_tiles[n].append(grouped)

        def quantise(n):
            if not 0 <= n < len(units):
                return
            kind, i, half = units[n]
            if half == 0:
                pool, name, rows = (x_mx, "x%d" % i, P) if kind == "x" else (w_mx, "w", BLOCK)
                codes = pool.tile([P, PASSES, rows], U32, name=name + "_codes", align_bytes=64)
                scales = pool.tile([P, PASSES, rows], U8, name=name + "_scales", align_bytes=64)
                mx_operands[kind, i] = (codes, scales)
            codes, scales = mx_operands[kind, i]
            codes_row = codes[:].rearrange("p q r -> p (q r)")
            scales_row = scales[:].rearrange("p q r -> p (q r)")
            for bank, grouped in enumerate(grouped_tiles.pop(n)):
                first = (half * UNIT_BANKS + bank) * BLOCK
                nc.vector.quantize_mx(
                    out=codes_row[:, first : first + BLOCK].bitcast(FP8X4),
                    scales=scales_row[:, first : first + BLOCK],
                    in_=grouped[:],
                )

        def multiply(piece):
            if piece is None:
                return
            n, m, count = piece
            w_codes, w_scales = mx_operands["w", n // X_PAIRS]
            if m == 0:
                acc = acc_psum.tile([P, 2, BLOCK], F32, name="acc")
                acc_banks[n] = acc
            for c in range(m, m + count):
                x_codes, x_scales = mx_operands["x", 2 * (n % X_PAIRS) + c]
                for q in range(PASSES):
                    nc.tensor.matmul_mx(
                        out=acc_banks[n][:, c, :],
                        lhsT=x_codes[:, q, :].bitcast(FP8X4),
                        lhsT_scale=x_scales[:, q, :],
                        rhs=w_codes[:, q, :].bitcast(FP8X4),
                        rhs_scale=w_scales[:, q, :],
                        start=(q == 0),
                        stop=(q == PASSES - 1),
                    )

        def add_bias(piece):
            if piece is None:
                return
            n, m, count = piece
            block = n // X_PAIRS
            u = work.tile([P, 2, BLOCK], F32, name="u")
            nc.vector.tensor_tensor(
                out=u[:, :count, :],
                in0=acc_banks[n][:, m : m + count, :],
                in1=bias[:, block * BLOCK : (block + 1) * BLOCK]
                .unsqueeze(1)
                .to_broadcast([P, count, BLOCK]),
                op=ALU.add,
            )
            biased[piece] = u

        def sum_squares(piece):
            if piece is None:
                return
            by_group = biased[piece][:].rearrange("p m (h d) -> p (m h) d", d=HEAD)
            squares = work.tile([P, GROUPS, HEAD], F32, name="squares")
            sums = stats.tile([P, GROUPS], F32, name="sums")
            for k in range(piece[2] * HEADS_IN_BLOCK):
                nc.scalar.activation(
                    out=squares[:, k, :], in_=by_group[:, k, :], func=ACT.Square,
                    accum_out=sums[:, k : k + 1],
                )
            square_sums[piece] = sums

        def invert_rms(piece):
            if piece is None:
                return
            groups = piece[2] * HEADS_IN_BLOCK
            inv_rms = stats.tile([P, GROUPS], F32, name="inv_rms")
            nc.scalar.activation(
                out=inv_rms[:, :groups], in_=square_sums.pop(piece)[:, :groups],
                func=ACT.Abs_reciprocal_sqrt, scale=1.0 / HEAD, bias=eps[:],
            )
            inverse_rms[piece] = inv_rms

        def multiply_by_tables(piece):
            if piece is None:
                return
            n, m, count = piece
            inv_rms = inverse_rms.pop(piece)
            pairs = biased.pop(piece)[:].rearrange("p m (h j i) -> p (m h) j i", h=HEADS_IN_BLOCK, i=2)
            product_tiles[piece] = []
            for c in range(2):
                product = work.tile([P, GROUPS, PAIRS, 2], F32, name="product%d" % c)
                for k in range(count * HEADS_IN_BLOCK):
                    token_tile = 2 * (n % X_PAIRS) + m + k // HEADS_IN_BLOCK
                    nc.vector.scalar_tensor_tensor(
                        out=product[:, k],
                        in0=pairs[:, k, :, c : c + 1].to_broadcast([P, PAIRS, 2]),
                        scalar=inv_rms[:, k : k + 1],
                        in1=table[c][:, token_tile],
                        op0=ALU.mult,
                        op1=ALU.mult,
                    )
                product_tiles[piece].append(product)

        def add_and_store(piece):
            if piece is None:
                return
            n, m, count = piece
            groups = count * HEADS_IN_BLOCK
            first, second = product_tiles.pop(piece)
            rotated = results.tile([P, GROUPS, HEAD], F32, name="rotated")
            nc.vector.tensor_tensor(
                out=rotated[:, :groups].rearrange("p k d -> p (k d)"),
                in0=first[:, :groups].rearrange("p k j i -> p (k j i)"),
                in1=second[:, :groups].rearrange("p k j i -> p (k j i)"),
                op=ALU.add,
            )
            token_tile, block = 2 * (n % X_PAIRS) + m, n // X_PAIRS
            nc.sync.dma_start(
                out=out_view[:, token_tile : token_tile + count, block * BLOCK : (block + 1) * BLOCK],
                in_=rotated[:, :groups].rearrange("p (m h) d -> p m (h d)", h=HEADS_IN_BLOCK),
            )

        for t in range(last_piece + ADD_LAG + 1):
            multiply(piece_of_step.get(t))
            transpose(t)
            sum_squares(piece_of_step.get(t - SQUARE_LAG))
            multiply_by_tables(piece_of_step.get(t - PRODUCT_LAG))
            add_and_store(piece_of_step.get(t - ADD_LAG))
            spread(t + 1, 0)
            invert_rms(piece_of_step.get(t - SQUARE_LAG))
            for part in range(1, len(SPREAD_PARTS)):
                spread(t + 1, part)
            quantise(t - QUANTISE_LAG)
            add_bias(piece_of_step.get(t))
            if t == first_piece + PRODUCT_LAG - 1:
                build_tables()
            regroup(t)
